import numpy as np
import ml_dtypes


def mxq(x, axis, fmt="e4m3"):
    dtype, down = {"e4m3": (ml_dtypes.float8_e4m3fn, 7), "e5m2": (ml_dtypes.float8_e5m2, 14)}[fmt]
    v = np.moveaxis(np.asarray(x, np.float32).astype(ml_dtypes.bfloat16).astype(np.float64), axis, -1)
    blocks = v.reshape(v.shape[:-1] + (-1, 32))
    amax = np.abs(blocks).max(-1, keepdims=True)
    byte = np.maximum(np.where(amax > 0, np.frexp(amax)[1] - 1 + 127, 0) - down, 1)
    scale = np.exp2(byte - 127.0)
    codes = (blocks / scale).astype(np.float32).astype(dtype).astype(np.float64)
    return np.moveaxis((codes * scale).reshape(v.shape), -1, axis)


WIDE = False


def mx_kscale(k):
    if not WIDE:
        return np.ones(k)
    levels = np.array([10, -10, 5, -5, 0])
    a = np.random.permutation(np.resize(levels, k // 512 * 4)).reshape(k // 512, 4)
    idx = np.arange(k)
    return np.exp2(a[idx // 512, idx % 128 // 32])


BF16 = ml_dtypes.bfloat16


def bf(x):
    return np.asarray(x, np.float32).astype(BF16)


def f64(x):
    return np.asarray(x).astype(np.float64)


E2M1 = np.array([0.0, 0.5, 1.0, 1.5, 2.0, 3.0, 4.0, 6.0, -0.0, -0.5, -1.0, -1.5, -2.0, -3.0, -4.0, -6.0])


def pack_weight(w, fmt):
    k, n = w.shape
    w = f64(bf(w)).reshape(k // 32, 32, n)
    amax = np.abs(w).max(1)
    if fmt == "e4m3":
        byte = np.frexp(amax)[1] - 1 + 127 - 7
    else:
        mant, ex = np.frexp(amax / 6.0)
        byte = np.where(mant > 0.5, ex, ex - 1) + 127
    byte = np.clip(np.where(amax > 0, byte, 1), 1, 254)
    scaled = (w * np.exp2(127.0 - byte)[:, None, :]).reshape(k, n).astype(np.float32)
    by_word = np.ascontiguousarray(scaled.reshape(k // 512, 128, 4, n).transpose(0, 1, 3, 2))
    if fmt == "e4m3":
        words = by_word.astype(ml_dtypes.float8_e4m3fn).view(np.uint8)
    else:
        c = by_word.astype(ml_dtypes.float4_e2m1fn).view(np.uint8) & 0xF
        words = c[..., 0::2] | (c[..., 1::2] << 4)
    return np.ascontiguousarray(words), np.ascontiguousarray(byte.astype(np.uint8).reshape(k // 512, 16, n))


def unpack_weight(words, scales, fmt):
    g, p, n, _ = words.shape
    if fmt == "e4m3":
        vals = np.ascontiguousarray(words).view(ml_dtypes.float8_e4m3fn).astype(np.float64)
    else:
        nib = np.empty((g, p, n, 4), np.uint8)
        nib[..., 0::2] = words & 0xF
        nib[..., 1::2] = words >> 4
        vals = E2M1[nib]
    vals = vals * np.repeat(np.exp2(scales.astype(np.float64) - 127.0), 8, axis=1)[..., None]
    return vals.transpose(0, 1, 3, 2).reshape(g * 512, n)

def pack4(w):
    words, scales = pack_weight(w, "e2m1")
    return words.reshape(words.shape[0], 128, -1), scales


def unpack4(words, scales):
    return unpack_weight(words.reshape(words.shape[0], 128, -1, 2), scales, "e2m1")


B, T, D, H, HD = 2, 512, 1024, 8, 128
E = H * HD
HALF = HD // 2


def rotate_half(u):
    return np.concatenate((-u[..., HALF:], u[..., :HALF]), axis=-1)


def setup_inputs():
    s = mx_kscale(D)
    x = bf(np.random.standard_normal((B, T, D)) * s)
    rope_cos = bf(np.random.random_sample((1, 1, T, HD)))
    rope_sin = bf(np.random.random_sample((1, 1, T, HD)))
    w = np.random.standard_normal((3 * E, D)) / np.sqrt(D) / s[None, :]
    words, scales = pack4(np.ascontiguousarray(w.T))
    qkv_b = bf(np.random.standard_normal(3 * E) * 0.3)
    return {"x": x,
            "rope_cos": rope_cos,
            "rope_sin": rope_sin,
            "qkv_w_words": words,
            "qkv_w_scales": scales,
            "qkv_b": qkv_b}


def reference(x, rope_cos, rope_sin, qkv_w_words, qkv_w_scales, qkv_b):
    qkv = (mxq(f64(x), 2, "e4m3") @ unpack4(qkv_w_words, qkv_w_scales)) + f64(qkv_b)
    qkv = qkv.reshape(B, T, 3, H, HD).transpose(2, 0, 3, 1, 4)
    q, k, v = qkv[0], qkv[1], qkv[2]
    cos = f64(rope_cos)[:, :, :T, :]
    sin = f64(rope_sin)[:, :, :T, :]
    q_rot = q * cos + rotate_half(q) * sin
    k_rot = k * cos + rotate_half(k) * sin
    return q_rot, k_rot, v

@@ -1,0 +1,215 @@
+from contextlib import ExitStack
+
+import concourse.mybir as mybir
+from concourse.masks import make_identity
+
+F32 = mybir.dt.float32
+BF16 = mybir.dt.bfloat16
+I32 = mybir.dt.int32
+U32 = mybir.dt.uint32
+U8 = mybir.dt.uint8
+FP8X4 = mybir.dt.float8_e4m3fn_x4
+FP4X4 = mybir.dt.float4_e2m1fn_x4
+MULT = mybir.AluOpType.mult
+ADD = mybir.AluOpType.add
+IDENTITY = mybir.ActivationFunctionType.Identity
+
+P = 128
+BATCH = 2
+TOKENS = 512
+K = 1024
+HEADS = 8
+HEAD_DIM = 128
+HALF = HEAD_DIM // 2
+STREAMS = 3
+COLS = STREAMS * HEADS * HEAD_DIM
+COL_TILES = COLS // P
+PACK = 4
+K_PASS = P * PACK
+PASSES = K // K_PASS
+TOK = TOKENS // P
+PAIRS = TOK // 2
+WORD_BYTES = 2
+FIRST_HEADS = 2
+
+FLOPS = 2 * BATCH * TOKENS * K * COLS
+
+
+def tile_causalselfattention_pa_kernel(
+    tc, x, rope_cos, rope_sin, qkv_w_words, qkv_w_scales, qkv_b, out_0, out_1, out_2
+):
+    nc = tc.nc
+    outs = (out_0, out_1, out_2)
+
+    with ExitStack() as ctx:
+        keep = ctx.enter_context(tc.tile_pool(name="keep", bufs=1))
+        feature_major = ctx.enter_context(tc.tile_pool(name="feature_major", bufs=2 * STREAMS))
+        products = ctx.enter_context(tc.tile_pool(name="products", bufs=4))
+        results = ctx.enter_context(tc.tile_pool(name="results", bufs=3 * STREAMS))
+        psum_feat = ctx.enter_context(tc.psum_pool(name="psum_feat", bufs=4))
+        psum_tok = ctx.enter_context(tc.psum_pool(name="psum_tok", bufs=4))
+        ctx.enter_context(tc.manual_schedule())
+
+        bias_rows = keep.tile([P, P], BF16, name="bias_rows")
+        nc.gpsimd.memset(bias_rows[:], 0.0)
+        ident = keep.tile([P, P], F32, name="ident")
+        make_identity(nc, ident[:])
+
+        w_planes = keep.tile([P, PASSES, COLS], U8, name="w_planes", align_bytes=64)
+        nc.vector.memset(w_planes[:].rearrange("p g n -> p (g n)").bitcast(I32), 0)
+
+        cos_rows = keep.tile([P, TOK, HEAD_DIM], BF16, name="cos_rows")
+        sin_rows = keep.tile([P, TOK, HEAD_DIM], BF16, name="sin_rows")
+        nc.scalar.dma_start(out=cos_rows[:], in_=rope_cos[0, 0].rearrange("(p j) d -> p j d", j=TOK))
+        nc.scalar.dma_start(out=sin_rows[:], in_=rope_sin[0, 0].rearrange("(p j) d -> p j d", j=TOK))
+        nc.scalar.dma_start(out=bias_rows[0:COL_TILES, :], in_=qkv_b.rearrange("(c d) -> c d", d=P))
+
+        x_rows = [keep.tile([P, TOK, K], BF16, name="x_rows%d" % b) for b in range(BATCH)]
+
+        def load_x(b):
+            rows = x[b].rearrange("(p j) k -> p j k", j=TOK)
+            for pair in range(PAIRS):
+                two = slice(2 * pair, 2 * pair + 2)
+                nc.sync.dma_start(out=x_rows[b][:, two, :], in_=rows[:, two, :])
+
+        def load_w_scales():
+            rows = qkv_w_scales.rearrange("g q n -> q g n")
+            for first in range(2 * PACK):
+                partition = 32 * (first // PACK) + first % PACK
+                nc.sync.dma_start(
+                    out=w_planes[partition:P:64, :, :].bitcast(I32),
+                    in_=rows[first : 16 : 2 * PACK, :, :].bitcast(I32),
+                )
+
+        w_words = keep.tile([P, PASSES, WORD_BYTES * COLS], U8, name="w_words", align_bytes=64)
+
+        def load_w_words(head_from, head_to):
+            some = slice(WORD_BYTES * HEAD_DIM * head_from, WORD_BYTES * HEAD_DIM * head_to)
+            for g in range(PASSES):
+                here = w_words[:, g, :].rearrange("p (s c) -> p s c", s=STREAMS)
+                there = qkv_w_words[g].rearrange("p (s c) -> p s c", s=STREAMS)
+                nc.sync.dma_start(out=here[:, :, some].bitcast(I32), in_=there[:, :, some].bitcast(I32))
+
+        load_x(0)
+        load_w_scales()
+        load_w_words(0, FIRST_HEADS)
+        load_x(1)
+        load_w_words(FIRST_HEADS, HEADS)
+
+        table_lo = keep.tile([P, TOK, 2, HALF], F32, name="table_lo")
+        table_hi = keep.tile([P, TOK, 2, HALF], F32, name="table_hi")
+        nc.scalar.copy(out=table_lo[:, :, 0, :], in_=cos_rows[:, :, 0:HALF])
+        nc.scalar.copy(out=table_lo[:, :, 1, :], in_=sin_rows[:, :, HALF:HEAD_DIM])
+        nc.scalar.mul(out=table_hi[:, :, 0, :], in_=sin_rows[:, :, 0:HALF], mul=-1.0)
+        nc.scalar.copy(out=table_hi[:, :, 1, :], in_=cos_rows[:, :, HALF:HEAD_DIM])
+
+        bias_rows_f32 = keep.tile([P, P], F32, name="bias_rows_f32")
+        nc.gpsimd.tensor_copy(out=bias_rows_f32[:], in_=bias_rows[:])
+
+        grouped = [
+            [keep.tile([P, PACK * TOKENS], BF16, name="grouped%d%d" % (b, g), align_bytes=64) for g in range(PASSES)]
+            for b in range(BATCH)
+        ]
+        x_codes = keep.tile([P, BATCH, PASSES, TOKENS], U32, name="x_codes", align_bytes=64)
+        x_planes = keep.tile([P, BATCH, PASSES, TOKENS], U8, name="x_planes", align_bytes=64)
+
+        def transpose_x(b, g, pair, copy):
+            words = x_rows[b][:].bitcast(F32)
+            xt = psum_feat.tile([P, 2, 2, P], F32, tag="bank", name="xt")
+            for jj in range(2):
+                for u in range(2):
+                    every_second = slice(K_PASS // 2 * g + u, K_PASS // 2 * (g + 1), 2)
+                    nc.tensor.transpose(xt[:, jj, u, :], words[:, 2 * pair + jj, every_second], ident[:])
+            pairs_of_k = grouped[b][g][:].bitcast(F32).rearrange("q (n u) -> q n u", u=2)
+            columns = slice(2 * P * pair, 2 * P * (pair + 1))
+            copy(
+                out=pairs_of_k[:, columns, :].rearrange("q (jj n) u -> q jj n u", jj=2),
+                in_=xt[:].rearrange("q jj u n -> q jj n u"),
+            )
+
+        def quantise_x(b, g, pair):
+            columns = slice(2 * P * pair, 2 * P * (pair + 1))
+            nc.vector.quantize_mx(
+                out=x_codes[:, b, g, columns].bitcast(FP8X4),
+                scales=x_planes[:, b, g, columns],
+                in_=grouped[b][g][:, PACK * 2 * P * pair : PACK * 2 * P * (pair + 1)],
+            )
+
+        for pair in range(PAIRS):
+            transpose_x(0, 0, pair, nc.vector.tensor_copy)
+            transpose_x(0, 1, pair, nc.scalar.copy)
+        for pair in range(PAIRS):
+            for g in range(PASSES):
+                quantise_x(0, g, pair)
+
+        bias_t = psum_tok.tile([P, P], F32, tag="bank", name="bias_t")
+        nc.tensor.transpose(bias_t[:], bias_rows_f32[:], ident[:])
+        bias_col = keep.tile([P, COL_TILES], F32, name="bias_col")
+        nc.scalar.copy(out=bias_col[:], in_=bias_t[:, 0:COL_TILES])
+
+        def project(b, h):
+            sums = []
+            for s in range(STREAMS):
+                c = s * HEADS + h
+                acc = psum_feat.tile([P, TOKENS], F32, tag="bank", name="acc")
+                for g in range(PASSES):
+                    nc.tensor.matmul_mx(
+                        out=acc[:],
+                        lhsT=w_words[:, g, WORD_BYTES * P * c : WORD_BYTES * P * (c + 1)].bitcast(FP4X4),
+                        lhsT_scale=w_planes[:, g, P * c : P * (c + 1)],
+                        rhs=x_codes[:, b, g, :].bitcast(FP8X4),
+                        rhs_scale=x_planes[:, b, g, :],
+                        start=(g == 0),
+                        stop=(g == PASSES - 1),
+                    )
+                sums.append(acc)
+            biased = []
+            for s in range(STREAMS):
+                c = s * HEADS + h
+                feat = feature_major.tile([P, TOKENS], F32, name="feat")
+                nc.scalar.activation(out=feat[:], in_=sums[s][:], func=IDENTITY, bias=bias_col[:, c : c + 1])
+                biased.append(feat)
+            return biased
+
+        def store(s, b, h, result):
+            nc.sync.dma_start(out=outs[s][b, h].rearrange("(p j) d -> p (j d)", j=TOK), in_=result)
+
+        def finish(b, h, biased):
+            token_major = []
+            for s in range(STREAMS):
+                tok = psum_tok.tile([P, TOK, HEAD_DIM], F32, tag="bank", name="tok")
+                for j in range(TOK):
+                    nc.tensor.transpose(tok[:, j, :], biased[s][:, P * j : P * (j + 1)], ident[:])
+                token_major.append(tok)
+
+            v_out = results.tile([P, TOK, HEAD_DIM], F32, tag="result", name="v_out")
+            nc.scalar.copy(out=v_out[:], in_=token_major[2][:])
+            store(2, b, h, v_out[:].rearrange("p j d -> p (j d)"))
+
+            twice = [P, TOK, 2, HALF]
+            for s in range(2):
+                tok = token_major[s]
+                from_lo = products.tile(twice, F32, name="from_lo")
+                from_hi = products.tile(twice, F32, name="from_hi")
+                nc.vector.tensor_tensor(
+                    out=from_lo[:], in0=tok[:, :, 0:HALF].unsqueeze(2).to_broadcast(twice), in1=table_lo[:], op=MULT
+                )
+                nc.vector.tensor_tensor(
+                    out=from_hi[:], in0=tok[:, :, HALF:HEAD_DIM].unsqueeze(2).to_broadcast(twice), in1=table_hi[:], op=MULT
+                )
+                rotated = results.tile(twice, F32, tag="result", name="rotated")
+                nc.gpsimd.tensor_tensor(out=rotated[:], in0=from_lo[:], in1=from_hi[:], op=ADD)
+                store(s, b, h, rotated[:].rearrange("p j w i -> p (j w i)"))
+
+        rounds = [(b, h) for b in range(BATCH) for h in range(HEADS)]
+        x_banks = [(g, pair) for pair in range(PAIRS) for g in range(PASSES)]
+
+        biased = project(*rounds[0])
+        for r in range(len(rounds)):
+            following = project(*rounds[r + 1]) if r + 1 < len(rounds) else None
+            finish(*rounds[r], biased)
+            if r < len(x_banks):
+                g, pair = x_banks[r]
+                transpose_x(1, g, pair, nc.scalar.copy)
+                quantise_x(1, g, pair)
+            biased = following

@@ -31,6 +31,7 @@ TOK = TOKENS // P
 PAIRS = TOK // 2
 WORD_BYTES = 2
 FIRST_HEADS = 2
+V_LAG = 2
 
 FLOPS = 2 * BATCH * TOKENS * K * COLS
 
@@ -44,8 +45,8 @@ def tile_causalselfattention_pa_kernel(
     with ExitStack() as ctx:
         keep = ctx.enter_context(tc.tile_pool(name="keep", bufs=1))
         feature_major = ctx.enter_context(tc.tile_pool(name="feature_major", bufs=2 * STREAMS))
-        products = ctx.enter_context(tc.tile_pool(name="products", bufs=4))
-        results = ctx.enter_context(tc.tile_pool(name="results", bufs=3 * STREAMS))
+        products = ctx.enter_context(tc.tile_pool(name="products", bufs=2))
+        results = ctx.enter_context(tc.tile_pool(name="results", bufs=3))
         psum_feat = ctx.enter_context(tc.psum_pool(name="psum_feat", bufs=4))
         psum_tok = ctx.enter_context(tc.psum_pool(name="psum_tok", bufs=4))
         ctx.enter_context(tc.manual_schedule())
@@ -68,18 +69,16 @@ def tile_causalselfattention_pa_kernel(
 
         def load_x(b):
             rows = x[b].rearrange("(p j) k -> p j k", j=TOK)
-            for pair in range(PAIRS):
-                two = slice(2 * pair, 2 * pair + 2)
-                nc.sync.dma_start(out=x_rows[b][:, two, :], in_=rows[:, two, :])
+            for g in range(PASSES):
+                of_pass = slice(K_PASS * g, K_PASS * (g + 1))
+                for pair in range(PAIRS):
+                    two = slice(2 * pair, 2 * pair + 2)
+                    nc.sync.dma_start(out=x_rows[b][:, two, of_pass], in_=rows[:, two, of_pass])
 
         def load_w_scales():
             rows = qkv_w_scales.rearrange("g q n -> q g n")
-            for first in range(2 * PACK):
-                partition = 32 * (first // PACK) + first % PACK
-                nc.sync.dma_start(
-                    out=w_planes[partition:P:64, :, :].bitcast(I32),
-                    in_=rows[first : 16 : 2 * PACK, :, :].bitcast(I32),
-                )
+            for r in range(PACK):
+                nc.sync.dma_start(out=w_planes[r:P:32, :, :].bitcast(I32), in_=rows[r : 4 * PACK : PACK, :, :].bitcast(I32))
 
         w_words = keep.tile([P, PASSES, WORD_BYTES * COLS], U8, name="w_words", align_bytes=64)
 
@@ -91,10 +90,10 @@ def tile_causalselfattention_pa_kernel(
                 nc.sync.dma_start(out=here[:, :, some].bitcast(I32), in_=there[:, :, some].bitcast(I32))
 
         load_x(0)
-        load_w_scales()
         load_w_words(0, FIRST_HEADS)
-        load_x(1)
+        load_w_scales()
         load_w_words(FIRST_HEADS, HEADS)
+        load_x(1)
 
         table_lo = keep.tile([P, TOK, 2, HALF], F32, name="table_lo")
         table_hi = keep.tile([P, TOK, 2, HALF], F32, name="table_hi")
@@ -137,22 +136,22 @@ def tile_causalselfattention_pa_kernel(
 
         for pair in range(PAIRS):
             transpose_x(0, 0, pair, nc.vector.tensor_copy)
-            transpose_x(0, 1, pair, nc.scalar.copy)
         for pair in range(PAIRS):
-            for g in range(PASSES):
-                quantise_x(0, g, pair)
+            transpose_x(0, 1, pair, nc.scalar.copy)
+            quantise_x(0, 0, pair)
+        for pair in range(PAIRS):
+            quantise_x(0, 1, pair)
 
         bias_t = psum_tok.tile([P, P], F32, tag="bank", name="bias_t")
         nc.tensor.transpose(bias_t[:], bias_rows_f32[:], ident[:])
         bias_col = keep.tile([P, COL_TILES], F32, name="bias_col")
         nc.scalar.copy(out=bias_col[:], in_=bias_t[:, 0:COL_TILES])
 
-        def project(b, h):
-            sums = []
-            for s in range(STREAMS):
-                c = s * HEADS + h
-                acc = psum_feat.tile([P, TOKENS], F32, tag="bank", name="acc")
-                for g in range(PASSES):
+        def project(units):
+            sums = [psum_feat.tile([P, TOKENS], F32, tag="bank", name="acc") for unit in units]
+            for g in range(PASSES):
+                for (s, b, h), acc in zip(units, sums):
+                    c = s * HEADS + h
                     nc.tensor.matmul_mx(
                         out=acc[:],
                         lhsT=w_words[:, g, WORD_BYTES * P * c : WORD_BYTES * P * (c + 1)].bitcast(FP4X4),
@@ -162,54 +161,64 @@ def tile_causalselfattention_pa_kernel(
                         start=(g == 0),
                         stop=(g == PASSES - 1),
                     )
-                sums.append(acc)
             biased = []
-            for s in range(STREAMS):
+            for (s, b, h), acc in zip(units, sums):
                 c = s * HEADS + h
                 feat = feature_major.tile([P, TOKENS], F32, name="feat")
-                nc.scalar.activation(out=feat[:], in_=sums[s][:], func=IDENTITY, bias=bias_col[:, c : c + 1])
+                nc.scalar.activation(out=feat[:], in_=acc[:], func=IDENTITY, bias=bias_col[:, c : c + 1])
                 biased.append(feat)
             return biased
 
-        def store(s, b, h, result):
+        def store(unit, result):
+            s, b, h = unit
             nc.sync.dma_start(out=outs[s][b, h].rearrange("(p j) d -> p (j d)", j=TOK), in_=result)
 
-        def finish(b, h, biased):
+        def finish(units, biased):
             token_major = []
-            for s in range(STREAMS):
+            for feat in biased:
                 tok = psum_tok.tile([P, TOK, HEAD_DIM], F32, tag="bank", name="tok")
                 for j in range(TOK):
-                    nc.tensor.transpose(tok[:, j, :], biased[s][:, P * j : P * (j + 1)], ident[:])
+                    nc.tensor.transpose(tok[:, j, :], feat[:, P * j : P * (j + 1)], ident[:])
                 token_major.append(tok)
 
-            v_out = results.tile([P, TOK, HEAD_DIM], F32, tag="result", name="v_out")
-            nc.scalar.copy(out=v_out[:], in_=token_major[2][:])
-            store(2, b, h, v_out[:].rearrange("p j d -> p (j d)"))
+            plain = [(unit, tok) for unit, tok in zip(units, token_major) if unit[0] == 2]
+            for unit, tok in plain:
+                v_out = results.tile([P, TOK, HEAD_DIM], F32, name="v_out")
+                nc.scalar.copy(out=v_out[:], in_=tok[:])
+                store(unit, v_out[:].rearrange("p j d -> p (j d)"))
 
-            twice = [P, TOK, 2, HALF]
-            for s in range(2):
-                tok = token_major[s]
-                from_lo = products.tile(twice, F32, name="from_lo")
-                from_hi = products.tile(twice, F32, name="from_hi")
-                nc.vector.tensor_tensor(
-                    out=from_lo[:], in0=tok[:, :, 0:HALF].unsqueeze(2).to_broadcast(twice), in1=table_lo[:], op=MULT
-                )
-                nc.vector.tensor_tensor(
-                    out=from_hi[:], in0=tok[:, :, HALF:HEAD_DIM].unsqueeze(2).to_broadcast(twice), in1=table_hi[:], op=MULT
-                )
-                rotated = results.tile(twice, F32, tag="result", name="rotated")
+            to_rotate = [(unit, tok) for unit, tok in zip(units, token_major) if unit[0] != 2]
+            if to_rotate:
+                twice = [P, TOK, 2, HALF]
+                from_lo = products.tile([P, len(to_rotate)] + twice[1:], F32, name="from_lo")
+                from_hi = products.tile([P, len(to_rotate)] + twice[1:], F32, name="from_hi")
+                rotated = results.tile([P, len(to_rotate)] + twice[1:], F32, name="rotated")
+                for i, (unit, tok) in enumerate(to_rotate):
+                    lo_twice = tok[:, :, 0:HALF].unsqueeze(2).to_broadcast(twice)
+                    hi_twice = tok[:, :, HALF:HEAD_DIM].unsqueeze(2).to_broadcast(twice)
+                    nc.vector.tensor_tensor(out=from_lo[:, i], in0=lo_twice, in1=table_lo[:], op=MULT)
+                    nc.vector.tensor_tensor(out=from_hi[:, i], in0=hi_twice, in1=table_hi[:], op=MULT)
                 nc.gpsimd.tensor_tensor(out=rotated[:], in0=from_lo[:], in1=from_hi[:], op=ADD)
-                store(s, b, h, rotated[:].rearrange("p j w i -> p (j w i)"))
+                for i, (unit, tok) in enumerate(to_rotate):
+                    store(unit, rotated[:, i].rearrange("p j w i -> p (j w i)"))
 
-        rounds = [(b, h) for b in range(BATCH) for h in range(HEADS)]
-        x_banks = [(g, pair) for pair in range(PAIRS) for g in range(PASSES)]
+        heads = [(b, h) for b in range(BATCH) for h in range(HEADS)]
+        steps = []
+        for r, (b, h) in enumerate(heads):
+            units = [(0, b, h), (1, b, h)]
+            if r >= V_LAG:
+                units.append((2,) + heads[r - V_LAG])
+            steps.append(units)
+        steps.append([(2,) + head for head in heads[len(heads) - V_LAG :]])
+        x_banks = [(g, pair) for g in range(PASSES) for pair in range(PAIRS)]
+        banks_a_step = len(x_banks) // V_LAG
 
-        biased = project(*rounds[0])
-        for r in range(len(rounds)):
-            following = project(*rounds[r + 1]) if r + 1 < len(rounds) else None
-            finish(*rounds[r], biased)
-            if r < len(x_banks):
-                g, pair = x_banks[r]
-                transpose_x(1, g, pair, nc.scalar.copy)
-                quantise_x(1, g, pair)
+        biased = project(steps[0])
+        for r in range(len(steps)):
+            following = project(steps[r + 1]) if r + 1 < len(steps) else None
+            finish(steps[r], biased)
+            if r < V_LAG:
+                for g, pair in x_banks[banks_a_step * r : banks_a_step * (r + 1)]:
+                    transpose_x(1, g, pair, nc.scalar.copy)
+                    quantise_x(1, g, pair)
             biased = following

@@ -30,8 +30,9 @@ PASSES = K // K_PASS
 TOK = TOKENS // P
 PAIRS = TOK // 2
 WORD_BYTES = 2
-FIRST_HEADS = 2
+HEADS_A_LOAD = 4
 V_LAG = 2
+GPSIMD_TOKENS = 3
 
 FLOPS = 2 * BATCH * TOKENS * K * COLS
 
@@ -65,7 +66,7 @@ def tile_causalselfattention_pa_kernel(
         nc.scalar.dma_start(out=sin_rows[:], in_=rope_sin[0, 0].rearrange("(p j) d -> p j d", j=TOK))
         nc.scalar.dma_start(out=bias_rows[0:COL_TILES, :], in_=qkv_b.rearrange("(c d) -> c d", d=P))
 
-        x_rows = [keep.tile([P, TOK, K], BF16, name="x_rows%d" % b) for b in range(BATCH)]
+        x_rows = [keep.tile([P, PASSES, TOK, K_PASS], BF16, name="x_rows%d" % b) for b in range(BATCH)]
 
         def load_x(b):
             rows = x[b].rearrange("(p j) k -> p j k", j=TOK)
@@ -73,34 +74,36 @@ def tile_causalselfattention_pa_kernel(
                 of_pass = slice(K_PASS * g, K_PASS * (g + 1))
                 for pair in range(PAIRS):
                     two = slice(2 * pair, 2 * pair + 2)
-                    nc.sync.dma_start(out=x_rows[b][:, two, of_pass], in_=rows[:, two, of_pass])
+                    nc.sync.dma_start(out=x_rows[b][:, g, two, :], in_=rows[:, two, of_pass])
 
         def load_w_scales():
             rows = qkv_w_scales.rearrange("g q n -> q g n")
             for r in range(PACK):
                 nc.sync.dma_start(out=w_planes[r:P:32, :, :].bitcast(I32), in_=rows[r : 4 * PACK : PACK, :, :].bitcast(I32))
 
-        w_words = keep.tile([P, PASSES, WORD_BYTES * COLS], U8, name="w_words", align_bytes=64)
+        head_bytes = WORD_BYTES * HEAD_DIM
+        w_words = [
+            keep.tile([P, PASSES, STREAMS, HEADS_A_LOAD * head_bytes], U8, name="w_words%d" % part, align_bytes=64)
+            for part in range(HEADS // HEADS_A_LOAD)
+        ]
 
-        def load_w_words(head_from, head_to):
-            some = slice(WORD_BYTES * HEAD_DIM * head_from, WORD_BYTES * HEAD_DIM * head_to)
+        def load_w_words(part):
+            some = slice(HEADS_A_LOAD * head_bytes * part, HEADS_A_LOAD * head_bytes * (part + 1))
             for g in range(PASSES):
-                here = w_words[:, g, :].rearrange("p (s c) -> p s c", s=STREAMS)
                 there = qkv_w_words[g].rearrange("p (s c) -> p s c", s=STREAMS)
-                nc.sync.dma_start(out=here[:, :, some].bitcast(I32), in_=there[:, :, some].bitcast(I32))
+                nc.sync.dma_start(out=w_words[part][:, g, :, :].bitcast(I32), in_=there[:, :, some].bitcast(I32))
 
         load_x(0)
-        load_w_words(0, FIRST_HEADS)
+        load_w_words(0)
         load_w_scales()
-        load_w_words(FIRST_HEADS, HEADS)
         load_x(1)
+        load_w_words(1)
 
-        table_lo = keep.tile([P, TOK, 2, HALF], F32, name="table_lo")
-        table_hi = keep.tile([P, TOK, 2, HALF], F32, name="table_hi")
-        nc.scalar.copy(out=table_lo[:, :, 0, :], in_=cos_rows[:, :, 0:HALF])
-        nc.scalar.copy(out=table_lo[:, :, 1, :], in_=sin_rows[:, :, HALF:HEAD_DIM])
-        nc.scalar.mul(out=table_hi[:, :, 0, :], in_=sin_rows[:, :, 0:HALF], mul=-1.0)
-        nc.scalar.copy(out=table_hi[:, :, 1, :], in_=cos_rows[:, :, HALF:HEAD_DIM])
+        tables = keep.tile([P, TOK, 2, 2, HALF], F32, name="tables")
+        nc.scalar.copy(out=tables[:, :, 0, 0, :], in_=cos_rows[:, :, 0:HALF])
+        nc.scalar.copy(out=tables[:, :, 0, 1, :], in_=sin_rows[:, :, HALF:HEAD_DIM])
+        nc.scalar.mul(out=tables[:, :, 1, 0, :], in_=sin_rows[:, :, 0:HALF], mul=-1.0)
+        nc.scalar.copy(out=tables[:, :, 1, 1, :], in_=cos_rows[:, :, HALF:HEAD_DIM])
 
         bias_rows_f32 = keep.tile([P, P], F32, name="bias_rows_f32")
         nc.gpsimd.tensor_copy(out=bias_rows_f32[:], in_=bias_rows[:])
@@ -112,13 +115,18 @@ def tile_causalselfattention_pa_kernel(
         x_codes = keep.tile([P, BATCH, PASSES, TOKENS], U32, name="x_codes", align_bytes=64)
         x_planes = keep.tile([P, BATCH, PASSES, TOKENS], U8, name="x_planes", align_bytes=64)
 
+        x_sorted = [keep.tile([P, PASSES, TOK, 2, P], F32, name="x_sorted%d" % b) for b in range(BATCH)]
+
+        def sort_x(b, g, pair, copy):
+            two = slice(2 * pair, 2 * pair + 2)
+            words = x_rows[b][:, g, two, :].bitcast(F32)
+            copy(out=x_sorted[b][:, g, two, :, :], in_=words.rearrange("t j (p u) -> t j u p", u=2))
+
         def transpose_x(b, g, pair, copy):
-            words = x_rows[b][:].bitcast(F32)
             xt = psum_feat.tile([P, 2, 2, P], F32, tag="bank", name="xt")
             for jj in range(2):
                 for u in range(2):
-                    every_second = slice(K_PASS // 2 * g + u, K_PASS // 2 * (g + 1), 2)
-                    nc.tensor.transpose(xt[:, jj, u, :], words[:, 2 * pair + jj, every_second], ident[:])
+                    nc.tensor.transpose(xt[:, jj, u, :], x_sorted[b][:, g, 2 * pair + jj, u, :], ident[:])
             pairs_of_k = grouped[b][g][:].bitcast(F32).rearrange("q (n u) -> q n u", u=2)
             columns = slice(2 * P * pair, 2 * P * (pair + 1))
             copy(
@@ -135,12 +143,18 @@ def tile_causalselfattention_pa_kernel(
             )
 
         for pair in range(PAIRS):
+            sort_x(0, 0, pair, nc.vector.tensor_copy)
+            sort_x(0, 1, pair, nc.scalar.copy)
+        for pair in range(PAIRS):
             transpose_x(0, 0, pair, nc.vector.tensor_copy)
         for pair in range(PAIRS):
             transpose_x(0, 1, pair, nc.scalar.copy)
             quantise_x(0, 0, pair)
         for pair in range(PAIRS):
             quantise_x(0, 1, pair)
+        for g in range(PASSES):
+            for pair in range(PAIRS):
+                sort_x(1, g, pair, nc.vector.tensor_copy)
 
         bias_t = psum_tok.tile([P, P], F32, tag="bank", name="bias_t")
         nc.tensor.transpose(bias_t[:], bias_rows_f32[:], ident[:])
@@ -152,9 +166,10 @@ def tile_causalselfattention_pa_kernel(
             for g in range(PASSES):
                 for (s, b, h), acc in zip(units, sums):
                     c = s * HEADS + h
+                    of_head = slice(head_bytes * (h % HEADS_A_LOAD), head_bytes * (h % HEADS_A_LOAD + 1))
                     nc.tensor.matmul_mx(
                         out=acc[:],
-                        lhsT=w_words[:, g, WORD_BYTES * P * c : WORD_BYTES * P * (c + 1)].bitcast(FP4X4),
+                        lhsT=w_words[h // HEADS_A_LOAD][:, g, s, of_head].bitcast(FP4X4),
                         lhsT_scale=w_planes[:, g, P * c : P * (c + 1)],
                         rhs=x_codes[:, b, g, :].bitcast(FP8X4),
                         rhs_scale=x_planes[:, b, g, :],
@@ -189,18 +204,26 @@ def tile_causalselfattention_pa_kernel(
 
             to_rotate = [(unit, tok) for unit, tok in zip(units, token_major) if unit[0] != 2]
             if to_rotate:
-                twice = [P, TOK, 2, HALF]
-                from_lo = products.tile([P, len(to_rotate)] + twice[1:], F32, name="from_lo")
-                from_hi = products.tile([P, len(to_rotate)] + twice[1:], F32, name="from_hi")
-                rotated = results.tile([P, len(to_rotate)] + twice[1:], F32, name="rotated")
-                for i, (unit, tok) in enumerate(to_rotate):
-                    lo_twice = tok[:, :, 0:HALF].unsqueeze(2).to_broadcast(twice)
-                    hi_twice = tok[:, :, HALF:HEAD_DIM].unsqueeze(2).to_broadcast(twice)
-                    nc.vector.tensor_tensor(out=from_lo[:, i], in0=lo_twice, in1=table_lo[:], op=MULT)
-                    nc.vector.tensor_tensor(out=from_hi[:, i], in0=hi_twice, in1=table_hi[:], op=MULT)
-                nc.gpsimd.tensor_tensor(out=rotated[:], in0=from_lo[:], in1=from_hi[:], op=ADD)
-                for i, (unit, tok) in enumerate(to_rotate):
-                    store(unit, rotated[:, i].rearrange("p j w i -> p (j w i)"))
+                parts = products.tile([P, len(to_rotate), TOK, 2, HEAD_DIM], F32, name="parts")
+                rotated = results.tile([P, len(to_rotate), TOK, HEAD_DIM], F32, name="rotated")
+                for n, (unit, tok) in enumerate(to_rotate):
+                    halves = tok[:].rearrange("p j (s i) -> p (j s) i", s=2)
+                    nc.vector.tensor_tensor(
+                        out=parts[:, n].rearrange("p j s (w i) -> p (j s) w i", w=2),
+                        in0=halves.unsqueeze(2).to_broadcast([P, TOK * 2, 2, HALF]),
+                        in1=tables[:].rearrange("p j s w i -> p (j s) w i"),
+                        op=MULT,
+                    )
+                most = slice(0, GPSIMD_TOKENS)
+                rest = slice(GPSIMD_TOKENS, TOK)
+                nc.gpsimd.tensor_tensor(
+                    out=rotated[:, :, most, :], in0=parts[:, :, most, 0, :], in1=parts[:, :, most, 1, :], op=ADD
+                )
+                nc.vector.tensor_tensor(
+                    out=rotated[:, :, rest, :], in0=parts[:, :, rest, 0, :], in1=parts[:, :, rest, 1, :], op=ADD
+                )
+                for n, (unit, tok) in enumerate(to_rotate):
+                    store(unit, rotated[:, n].rearrange("p j d -> p (j d)"))
 
         heads = [(b, h) for b in range(BATCH) for h in range(HEADS)]
         steps = []

@@ -32,7 +32,6 @@ PAIRS = TOK // 2
 WORD_BYTES = 2
 HEADS_A_LOAD = 4
 V_LAG = 2
-GPSIMD_TOKENS = 3
 
 FLOPS = 2 * BATCH * TOKENS * K * COLS
 
@@ -60,11 +59,13 @@ def tile_causalselfattention_pa_kernel(
         w_planes = keep.tile([P, PASSES, COLS], U8, name="w_planes", align_bytes=64)
         nc.vector.memset(w_planes[:].rearrange("p g n -> p (g n)").bitcast(I32), 0)
 
+        nc.scalar.dma_start(out=bias_rows[0:COL_TILES, :], in_=qkv_b.rearrange("(c d) -> c d", d=P))
         cos_rows = keep.tile([P, TOK, HEAD_DIM], BF16, name="cos_rows")
         sin_rows = keep.tile([P, TOK, HEAD_DIM], BF16, name="sin_rows")
-        nc.scalar.dma_start(out=cos_rows[:], in_=rope_cos[0, 0].rearrange("(p j) d -> p j d", j=TOK))
-        nc.scalar.dma_start(out=sin_rows[:], in_=rope_sin[0, 0].rearrange("(p j) d -> p j d", j=TOK))
-        nc.scalar.dma_start(out=bias_rows[0:COL_TILES, :], in_=qkv_b.rearrange("(c d) -> c d", d=P))
+
+        def load_tables():
+            nc.sync.dma_start(out=cos_rows[:], in_=rope_cos[0, 0].rearrange("(p j) d -> p j d", j=TOK))
+            nc.sync.dma_start(out=sin_rows[:], in_=rope_sin[0, 0].rearrange("(p j) d -> p j d", j=TOK))
 
         x_rows = [keep.tile([P, PASSES, TOK, K_PASS], BF16, name="x_rows%d" % b) for b in range(BATCH)]
 
@@ -94,19 +95,21 @@ def tile_causalselfattention_pa_kernel(
                 nc.sync.dma_start(out=w_words[part][:, g, :, :].bitcast(I32), in_=there[:, :, some].bitcast(I32))
 
         load_x(0)
-        load_w_words(0)
         load_w_scales()
+        load_w_words(0)
+        load_tables()
         load_x(1)
         load_w_words(1)
 
-        tables = keep.tile([P, TOK, 2, 2, HALF], F32, name="tables")
-        nc.scalar.copy(out=tables[:, :, 0, 0, :], in_=cos_rows[:, :, 0:HALF])
-        nc.scalar.copy(out=tables[:, :, 0, 1, :], in_=sin_rows[:, :, HALF:HEAD_DIM])
-        nc.scalar.mul(out=tables[:, :, 1, 0, :], in_=sin_rows[:, :, 0:HALF], mul=-1.0)
-        nc.scalar.copy(out=tables[:, :, 1, 1, :], in_=cos_rows[:, :, HALF:HEAD_DIM])
-
         bias_rows_f32 = keep.tile([P, P], F32, name="bias_rows_f32")
         nc.gpsimd.tensor_copy(out=bias_rows_f32[:], in_=bias_rows[:])
+        tables = keep.tile([P, TOK, 2, 2, HALF], F32, name="tables")
+        lo_cols = slice(0, HALF)
+        hi_cols = slice(HALF, HEAD_DIM)
+        nc.gpsimd.tensor_scalar(out=tables[:, :, 0, 0, :], in0=cos_rows[:, :, lo_cols], scalar1=1.0, scalar2=0.0, op0=MULT, op1=ADD)
+        nc.gpsimd.tensor_scalar(out=tables[:, :, 0, 1, :], in0=sin_rows[:, :, hi_cols], scalar1=1.0, scalar2=0.0, op0=MULT, op1=ADD)
+        nc.gpsimd.tensor_scalar(out=tables[:, :, 1, 0, :], in0=sin_rows[:, :, lo_cols], scalar1=-1.0, scalar2=0.0, op0=MULT, op1=ADD)
+        nc.gpsimd.tensor_scalar(out=tables[:, :, 1, 1, :], in0=cos_rows[:, :, hi_cols], scalar1=1.0, scalar2=0.0, op0=MULT, op1=ADD)
 
         grouped = [
             [keep.tile([P, PACK * TOKENS], BF16, name="grouped%d%d" % (b, g), align_bytes=64) for g in range(PASSES)]
@@ -188,7 +191,7 @@ def tile_causalselfattention_pa_kernel(
             s, b, h = unit
             nc.sync.dma_start(out=outs[s][b, h].rearrange("(p j) d -> p (j d)", j=TOK), in_=result)
 
-        def finish(units, biased):
+        def finish(units, biased, adder):
             token_major = []
             for feat in biased:
                 tok = psum_tok.tile([P, TOK, HEAD_DIM], F32, tag="bank", name="tok")
@@ -204,24 +207,17 @@ def tile_causalselfattention_pa_kernel(
 
             to_rotate = [(unit, tok) for unit, tok in zip(units, token_major) if unit[0] != 2]
             if to_rotate:
-                parts = products.tile([P, len(to_rotate), TOK, 2, HEAD_DIM], F32, name="parts")
+                parts = products.tile([P, 2, len(to_rotate), TOK, HEAD_DIM], F32, name="parts")
                 rotated = results.tile([P, len(to_rotate), TOK, HEAD_DIM], F32, name="rotated")
                 for n, (unit, tok) in enumerate(to_rotate):
-                    halves = tok[:].rearrange("p j (s i) -> p (j s) i", s=2)
+                    halves = tok[:].rearrange("p j (s i) -> p j s i", s=2)
                     nc.vector.tensor_tensor(
-                        out=parts[:, n].rearrange("p j s (w i) -> p (j s) w i", w=2),
-                        in0=halves.unsqueeze(2).to_broadcast([P, TOK * 2, 2, HALF]),
-                        in1=tables[:].rearrange("p j s w i -> p (j s) w i"),
+                        out=parts[:, :, n].rearrange("p s j (w i) -> p j s w i", w=2),
+                        in0=halves.unsqueeze(3).to_broadcast([P, TOK, 2, 2, HALF]),
+                        in1=tables[:],
                         op=MULT,
                     )
-                most = slice(0, GPSIMD_TOKENS)
-                rest = slice(GPSIMD_TOKENS, TOK)
-                nc.gpsimd.tensor_tensor(
-                    out=rotated[:, :, most, :], in0=parts[:, :, most, 0, :], in1=parts[:, :, most, 1, :], op=ADD
-                )
-                nc.vector.tensor_tensor(
-                    out=rotated[:, :, rest, :], in0=parts[:, :, rest, 0, :], in1=parts[:, :, rest, 1, :], op=ADD
-                )
+                adder.tensor_tensor(out=rotated[:], in0=parts[:, 0], in1=parts[:, 1], op=ADD)
                 for n, (unit, tok) in enumerate(to_rotate):
                     store(unit, rotated[:, n].rearrange("p j d -> p (j d)"))
 
@@ -239,7 +235,7 @@ def tile_causalselfattention_pa_kernel(
         biased = project(steps[0])
         for r in range(len(steps)):
             following = project(steps[r + 1]) if r + 1 < len(steps) else None
-            finish(steps[r], biased)
+            finish(steps[r], biased, nc.vector if r + 1 >= len(heads) else nc.gpsimd)
             if r < V_LAG:
                 for g, pair in x_banks[banks_a_step * r : banks_a_step * (r + 1)]:
                     transpose_x(1, g, pair, nc.scalar.copy)

@@ -45,7 +45,8 @@ def tile_causalselfattention_pa_kernel(
     with ExitStack() as ctx:
         keep = ctx.enter_context(tc.tile_pool(name="keep", bufs=1))
         feature_major = ctx.enter_context(tc.tile_pool(name="feature_major", bufs=2 * STREAMS))
-        products = ctx.enter_context(tc.tile_pool(name="products", bufs=2))
+        products = ctx.enter_context(tc.tile_pool(name="products", bufs=4))
+        sums_pool = ctx.enter_context(tc.tile_pool(name="sums_pool", bufs=6))
         results = ctx.enter_context(tc.tile_pool(name="results", bufs=3))
         psum_feat = ctx.enter_context(tc.psum_pool(name="psum_feat", bufs=4))
         psum_tok = ctx.enter_context(tc.psum_pool(name="psum_tok", bufs=4))
@@ -191,7 +192,7 @@ def tile_causalselfattention_pa_kernel(
             s, b, h = unit
             nc.sync.dma_start(out=outs[s][b, h].rearrange("(p j) d -> p (j d)", j=TOK), in_=result)
 
-        def finish(units, biased, adder):
+        def finish(units, biased, adders):
             token_major = []
             for feat in biased:
                 tok = psum_tok.tile([P, TOK, HEAD_DIM], F32, tag="bank", name="tok")
@@ -206,20 +207,21 @@ def tile_causalselfattention_pa_kernel(
                 store(unit, v_out[:].rearrange("p j d -> p (j d)"))
 
             to_rotate = [(unit, tok) for unit, tok in zip(units, token_major) if unit[0] != 2]
-            if to_rotate:
-                parts = products.tile([P, 2, len(to_rotate), TOK, HEAD_DIM], F32, name="parts")
-                rotated = results.tile([P, len(to_rotate), TOK, HEAD_DIM], F32, name="rotated")
-                for n, (unit, tok) in enumerate(to_rotate):
-                    halves = tok[:].rearrange("p j (s i) -> p j s i", s=2)
-                    nc.vector.tensor_tensor(
-                        out=parts[:, :, n].rearrange("p s j (w i) -> p j s w i", w=2),
-                        in0=halves.unsqueeze(3).to_broadcast([P, TOK, 2, 2, HALF]),
-                        in1=tables[:],
-                        op=MULT,
-                    )
+            waiting = []
+            for (unit, tok), adder in zip(to_rotate, adders):
+                parts = products.tile([P, 2, TOK, HEAD_DIM], F32, name="parts")
+                halves = tok[:].rearrange("p j (s i) -> p j s i", s=2)
+                nc.vector.tensor_tensor(
+                    out=parts[:].rearrange("p s j (w i) -> p j s w i", w=2),
+                    in0=halves.unsqueeze(3).to_broadcast([P, TOK, 2, 2, HALF]),
+                    in1=tables[:],
+                    op=MULT,
+                )
+                waiting.append((unit, parts, adder))
+            for unit, parts, adder in waiting:
+                rotated = sums_pool.tile([P, TOK, HEAD_DIM], F32, name="rotated")
                 adder.tensor_tensor(out=rotated[:], in0=parts[:, 0], in1=parts[:, 1], op=ADD)
-                for n, (unit, tok) in enumerate(to_rotate):
-                    store(unit, rotated[:, n].rearrange("p j d -> p (j d)"))
+                store(unit, rotated[:].rearrange("p j d -> p (j d)"))
 
         heads = [(b, h) for b in range(BATCH) for h in range(HEADS)]
         steps = []
@@ -235,7 +237,7 @@ def tile_causalselfattention_pa_kernel(
         biased = project(steps[0])
         for r in range(len(steps)):
             following = project(steps[r + 1]) if r + 1 < len(steps) else None
-            finish(steps[r], biased, nc.vector if r + 1 >= len(heads) else nc.gpsimd)
+            finish(steps[r], biased, (nc.gpsimd, nc.vector if r + 1 >= len(heads) else nc.gpsimd))
             if r < V_LAG:
                 for g, pair in x_banks[banks_a_step * r : banks_a_step * (r + 1)]:
                     transpose_x(1, g, pair, nc.scalar.copy)

@@ -30,7 +30,7 @@ PASSES = K // K_PASS
 TOK = TOKENS // P
 PAIRS = TOK // 2
 WORD_BYTES = 2
-HEADS_A_LOAD = 4
+HEADS_A_LOAD = 2
 V_LAG = 2
 
 FLOPS = 2 * BATCH * TOKENS * K * COLS
@@ -99,8 +99,10 @@ def tile_causalselfattention_pa_kernel(
         load_w_scales()
         load_w_words(0)
         load_tables()
-        load_x(1)
         load_w_words(1)
+        load_x(1)
+        load_w_words(2)
+        load_w_words(3)
 
         bias_rows_f32 = keep.tile([P, P], F32, name="bias_rows_f32")
         nc.gpsimd.tensor_copy(out=bias_rows_f32[:], in_=bias_rows[:])
@@ -188,9 +190,9 @@ def tile_causalselfattention_pa_kernel(
                 biased.append(feat)
             return biased
 
-        def store(unit, result):
+        def store(unit, result, queue):
             s, b, h = unit
-            nc.sync.dma_start(out=outs[s][b, h].rearrange("(p j) d -> p (j d)", j=TOK), in_=result)
+            queue.dma_start(out=outs[s][b, h].rearrange("(p j) d -> p (j d)", j=TOK), in_=result)
 
         def finish(units, biased, adders):
             token_major = []
@@ -204,7 +206,7 @@ def tile_causalselfattention_pa_kernel(
             for unit, tok in plain:
                 v_out = results.tile([P, TOK, HEAD_DIM], F32, name="v_out")
                 nc.scalar.copy(out=v_out[:], in_=tok[:])
-                store(unit, v_out[:].rearrange("p j d -> p (j d)"))
+                store(unit, v_out[:].rearrange("p j d -> p (j d)"), nc.scalar)
 
             to_rotate = [(unit, tok) for unit, tok in zip(units, token_major) if unit[0] != 2]
             waiting = []
@@ -221,7 +223,7 @@ def tile_causalselfattention_pa_kernel(
             for unit, parts, adder in waiting:
                 rotated = sums_pool.tile([P, TOK, HEAD_DIM], F32, name="rotated")
                 adder.tensor_tensor(out=rotated[:], in0=parts[:, 0], in1=parts[:, 1], op=ADD)
-                store(unit, rotated[:].rearrange("p j d -> p (j d)"))
+                store(unit, rotated[:].rearrange("p j d -> p (j d)"), nc.sync)
 
         heads = [(b, h) for b in range(BATCH) for h in range(HEADS)]
         steps = []

@@ -99,8 +99,8 @@ def tile_causalselfattention_pa_kernel(
         load_w_scales()
         load_w_words(0)
         load_tables()
-        load_w_words(1)
         load_x(1)
+        load_w_words(1)
         load_w_words(2)
         load_w_words(3)
 

@@ -31,6 +31,8 @@ TOK = TOKENS // P
 PAIRS = TOK // 2
 WORD_BYTES = 2
 HEADS_A_LOAD = 2
+WARM_FIRST = 8
+WARM_BETWEEN = 1
 V_LAG = 2
 
 FLOPS = 2 * BATCH * TOKENS * K * COLS
@@ -52,6 +54,15 @@ def tile_causalselfattention_pa_kernel(
         psum_tok = ctx.enter_context(tc.psum_pool(name="psum_tok", bufs=4))
         ctx.enter_context(tc.manual_schedule())
 
+        zeros = keep.tile([P, TOKENS], BF16, name="zeros")
+        nc.gpsimd.memset(zeros[:], 0.0)
+
+        def keep_warm(count):
+            for n in range(count):
+                unread = psum_tok.tile([P, TOKENS], F32, tag="bank", name="unread")
+                nc.tensor.matmul(out=unread[:], lhsT=zeros[:, 0:P], rhs=zeros[:], start=True, stop=True)
+
+        keep_warm(WARM_FIRST)
         bias_rows = keep.tile([P, P], BF16, name="bias_rows")
         nc.gpsimd.memset(bias_rows[:], 0.0)
         ident = keep.tile([P, P], F32, name="ident")
@@ -153,8 +164,10 @@ def tile_causalselfattention_pa_kernel(
             sort_x(0, 1, pair, nc.scalar.copy)
         for pair in range(PAIRS):
             transpose_x(0, 0, pair, nc.vector.tensor_copy)
+            keep_warm(WARM_BETWEEN)
         for pair in range(PAIRS):
             transpose_x(0, 1, pair, nc.scalar.copy)
+            keep_warm(WARM_BETWEEN)
             quantise_x(0, 0, pair)
         for pair in range(PAIRS):
             quantise_x(0, 1, pair)

@@ -31,6 +31,7 @@ TOK = TOKENS // P
 PAIRS = TOK // 2
 WORD_BYTES = 2
 HEADS_A_LOAD = 2
+WIDE_HEADS = 4
 WARM_FIRST = 8
 WARM_BETWEEN = 1
 V_LAG = 2
@@ -50,6 +51,7 @@ def tile_causalselfattention_pa_kernel(
         products = ctx.enter_context(tc.tile_pool(name="products", bufs=4))
         sums_pool = ctx.enter_context(tc.tile_pool(name="sums_pool", bufs=6))
         results = ctx.enter_context(tc.tile_pool(name="results", bufs=3))
+        v_pool = ctx.enter_context(tc.tile_pool(name="v_pool", bufs=2))
         psum_feat = ctx.enter_context(tc.psum_pool(name="psum_feat", bufs=4))
         psum_tok = ctx.enter_context(tc.psum_pool(name="psum_tok", bufs=4))
         ctx.enter_context(tc.manual_schedule())
@@ -72,6 +74,11 @@ def tile_causalselfattention_pa_kernel(
         nc.vector.memset(w_planes[:].rearrange("p g n -> p (g n)").bitcast(I32), 0)
 
         nc.scalar.dma_start(out=bias_rows[0:COL_TILES, :], in_=qkv_b.rearrange("(c d) -> c d", d=P))
+        wide = WIDE_HEADS * HEAD_DIM
+        v_bias_row = keep.tile([P, wide], BF16, name="v_bias_row")
+        nc.vector.memset(v_bias_row[:], 0.0)
+        ones = keep.tile([P, P], BF16, name="ones")
+        nc.vector.memset(ones[:], 1.0)
         cos_rows = keep.tile([P, TOK, HEAD_DIM], BF16, name="cos_rows")
         sin_rows = keep.tile([P, TOK, HEAD_DIM], BF16, name="sin_rows")
 
@@ -100,18 +107,27 @@ def tile_causalselfattention_pa_kernel(
             for part in range(HEADS // HEADS_A_LOAD)
         ]
 
+        w_wide = keep.tile([P, PASSES, WIDE_HEADS * head_bytes], U8, name="w_wide", align_bytes=64)
+
         def load_w_words(part):
             some = slice(HEADS_A_LOAD * head_bytes * part, HEADS_A_LOAD * head_bytes * (part + 1))
+            streams = STREAMS if HEADS_A_LOAD * part < HEADS - WIDE_HEADS else STREAMS - 1
             for g in range(PASSES):
                 there = qkv_w_words[g].rearrange("p (s c) -> p s c", s=STREAMS)
-                nc.sync.dma_start(out=w_words[part][:, g, :, :].bitcast(I32), in_=there[:, :, some].bitcast(I32))
+                nc.sync.dma_start(out=w_words[part][:, g, 0:streams, :].bitcast(I32), in_=there[:, 0:streams, some].bitcast(I32))
+
+        def load_w_wide():
+            for g in range(PASSES):
+                nc.sync.dma_start(out=w_wide[:, g, :].bitcast(I32), in_=qkv_w_words[g][:, WORD_BYTES * (COLS - wide) : WORD_BYTES * COLS].bitcast(I32))
 
         load_x(0)
         load_w_scales()
         load_w_words(0)
         load_tables()
+        nc.sync.dma_start(out=v_bias_row[0:1, :], in_=qkv_b[COLS - wide : COLS].rearrange("(o n) -> o n", o=1))
         load_x(1)
         load_w_words(1)
+        load_w_wide()
         load_w_words(2)
         load_w_words(3)
 
@@ -238,20 +254,53 @@ def tile_causalselfattention_pa_kernel(
                 adder.tensor_tensor(out=rotated[:], in0=parts[:, 0], in1=parts[:, 1], op=ADD)
                 store(unit, rotated[:].rearrange("p j d -> p (j d)"), nc.sync)
 
+        def project_wide(b, j):
+            acc = psum_feat.tile([P, WIDE_HEADS, HEAD_DIM], F32, tag="bank", name="wide_acc")
+            tokens = slice(P * j, P * (j + 1))
+            for g in range(PASSES):
+                nc.tensor.matmul_mx(
+                    out=acc[:].rearrange("p h d -> p (h d)"),
+                    lhsT=x_codes[:, b, g, tokens].bitcast(FP8X4),
+                    lhsT_scale=x_planes[:, b, g, tokens],
+                    rhs=w_wide[:, g, :].bitcast(FP4X4),
+                    rhs_scale=w_planes[:, g, COLS - wide : COLS],
+                    start=(g == 0),
+                    stop=(g == PASSES - 1),
+                )
+            return acc
+
+        wide_groups = {}
+
+        def finish_wide(b, j, acc):
+            if j == 0:
+                wide_group = v_pool.tile([P, WIDE_HEADS, TOK, HEAD_DIM], F32, name="wide_group")
+                wide_groups[b] = wide_group
+            group = wide_groups[b]
+            nc.vector.tensor_tensor(out=group[:, :, j, :], in0=acc[:], in1=v_bias[:], op=ADD)
+            there = out_2[b, HEADS - WIDE_HEADS : HEADS]
+            if b == BATCH - 1:
+                nc.sync.dma_start(out=there.rearrange("h (p j) d -> p h j d", j=TOK)[:, :, j, :], in_=group[:, :, j, :])
+            elif j == TOK - 1:
+                nc.sync.dma_start(out=there.rearrange("h (p j) d -> p h (j d)", j=TOK), in_=group[:].rearrange("p h j d -> p h (j d)"))
+
         heads = [(b, h) for b in range(BATCH) for h in range(HEADS)]
-        steps = []
-        for r, (b, h) in enumerate(heads):
-            units = [(0, b, h), (1, b, h)]
-            if r >= V_LAG:
-                units.append((2,) + heads[r - V_LAG])
-            steps.append(units)
-        steps.append([(2,) + head for head in heads[len(heads) - V_LAG :]])
+        steps = [[(0, b, h), (1, b, h)] for b, h in heads] + [[]]
+        wide_of_step = [[] for step in steps]
+        for n in range(BATCH * TOK):
+            wide_of_step[2 * n + 1].append((n // TOK, n % TOK))
+            steps[2 * n + 2].append((2, n // TOK, n % TOK))
         x_banks = [(g, pair) for g in range(PASSES) for pair in range(PAIRS)]
         banks_a_step = len(x_banks) // V_LAG
 
         biased = project(steps[0])
+        spread = psum_tok.tile([P, wide], F32, tag="bank", name="spread")
+        nc.tensor.matmul(out=spread[:], lhsT=ones[:], rhs=v_bias_row[:], start=True, stop=True)
+        v_bias = keep.tile([P, WIDE_HEADS, HEAD_DIM], F32, name="v_bias")
+        nc.scalar.copy(out=v_bias[:].rearrange("p h d -> p (h d)"), in_=spread[:])
         for r in range(len(steps)):
             following = project(steps[r + 1]) if r + 1 < len(steps) else None
+            for b, j in wide_of_step[r]:
+                finish_wide(b, j, project_wide(b, j))
             finish(steps[r], biased, (nc.gpsimd, nc.vector if r + 1 >= len(heads) else nc.gpsimd))
             if r < V_LAG:
                 for g, pair in x_banks[banks_a_step * r : banks_a_step * (r + 1)]:

@@ -133,13 +133,16 @@ def tile_causalselfattention_pa_kernel(
 
         bias_rows_f32 = keep.tile([P, P], F32, name="bias_rows_f32")
         nc.gpsimd.tensor_copy(out=bias_rows_f32[:], in_=bias_rows[:])
-        tables = keep.tile([P, TOK, 2, 2, HALF], F32, name="tables")
-        lo_cols = slice(0, HALF)
-        hi_cols = slice(HALF, HEAD_DIM)
-        nc.gpsimd.tensor_scalar(out=tables[:, :, 0, 0, :], in0=cos_rows[:, :, lo_cols], scalar1=1.0, scalar2=0.0, op0=MULT, op1=ADD)
-        nc.gpsimd.tensor_scalar(out=tables[:, :, 0, 1, :], in0=sin_rows[:, :, hi_cols], scalar1=1.0, scalar2=0.0, op0=MULT, op1=ADD)
-        nc.gpsimd.tensor_scalar(out=tables[:, :, 1, 0, :], in0=sin_rows[:, :, lo_cols], scalar1=-1.0, scalar2=0.0, op0=MULT, op1=ADD)
-        nc.gpsimd.tensor_scalar(out=tables[:, :, 1, 1, :], in0=cos_rows[:, :, hi_cols], scalar1=1.0, scalar2=0.0, op0=MULT, op1=ADD)
+
+        tables = keep.tile([P, TOK, 2, 2, HALF], BF16, name="tables")
+
+        def make_tables():
+            lo_cols = slice(0, HALF)
+            hi_cols = slice(HALF, HEAD_DIM)
+            nc.vector.tensor_copy(out=tables[:, :, 0, 0, :], in_=cos_rows[:, :, lo_cols])
+            nc.vector.tensor_copy(out=tables[:, :, 0, 1, :], in_=sin_rows[:, :, hi_cols])
+            nc.vector.tensor_scalar(out=tables[:, :, 1, 0, :], in0=sin_rows[:, :, lo_cols], scalar1=-1.0, scalar2=0.0, op0=MULT, op1=ADD)
+            nc.vector.tensor_copy(out=tables[:, :, 1, 1, :], in_=cos_rows[:, :, hi_cols])
 
         grouped = [
             [keep.tile([P, PACK * TOKENS], BF16, name="grouped%d%d" % (b, g), align_bytes=64) for g in range(PASSES)]
@@ -187,6 +190,7 @@ def tile_causalselfattention_pa_kernel(
             quantise_x(0, 0, pair)
         for pair in range(PAIRS):
             quantise_x(0, 1, pair)
+        make_tables()
         for g in range(PASSES):
             for pair in range(PAIRS):
                 sort_x(1, g, pair, nc.vector.tensor_copy)

@@ -34,6 +34,7 @@ HEADS_A_LOAD = 2
 WIDE_HEADS = 4
 WARM_FIRST = 8
 WARM_BETWEEN = 1
+WARM_LAST = 3
 V_LAG = 2
 
 FLOPS = 2 * BATCH * TOKENS * K * COLS
@@ -190,6 +191,7 @@ def tile_causalselfattention_pa_kernel(
             quantise_x(0, 0, pair)
         for pair in range(PAIRS):
             quantise_x(0, 1, pair)
+        keep_warm(WARM_LAST)
         make_tables()
         for g in range(PASSES):
             for pair in range(PAIRS):

from contextlib import ExitStack

import concourse.mybir as mybir
from concourse.masks import make_identity

F32 = mybir.dt.float32
BF16 = mybir.dt.bfloat16
I32 = mybir.dt.int32
U32 = mybir.dt.uint32
U8 = mybir.dt.uint8
FP8X4 = mybir.dt.float8_e4m3fn_x4
FP4X4 = mybir.dt.float4_e2m1fn_x4
MULT = mybir.AluOpType.mult
ADD = mybir.AluOpType.add
IDENTITY = mybir.ActivationFunctionType.Identity

P = 128
BATCH = 2
TOKENS = 512
K = 1024
HEADS = 8
HEAD_DIM = 128
HALF = HEAD_DIM // 2
STREAMS = 3
COLS = STREAMS * HEADS * HEAD_DIM
COL_TILES = COLS // P
PACK = 4
K_PASS = P * PACK
PASSES = K // K_PASS
TOK = TOKENS // P
PAIRS = TOK // 2
WORD_BYTES = 2
HEADS_A_LOAD = 2
WIDE_HEADS = 4
WARM_FIRST = 8
WARM_BETWEEN = 1
WARM_LAST = 3
V_LAG = 2

FLOPS = 2 * BATCH * TOKENS * K * COLS


def tile_causalselfattention_pa_kernel(
    tc, x, rope_cos, rope_sin, qkv_w_words, qkv_w_scales, qkv_b, out_0, out_1, out_2
):
    nc = tc.nc
    outs = (out_0, out_1, out_2)

    with ExitStack() as ctx:
        keep = ctx.enter_context(tc.tile_pool(name="keep", bufs=1))
        feature_major = ctx.enter_context(tc.tile_pool(name="feature_major", bufs=2 * STREAMS))
        products = ctx.enter_context(tc.tile_pool(name="products", bufs=4))
        sums_pool = ctx.enter_context(tc.tile_pool(name="sums_pool", bufs=6))
        results = ctx.enter_context(tc.tile_pool(name="results", bufs=3))
        v_pool = ctx.enter_context(tc.tile_pool(name="v_pool", bufs=2))
        psum_feat = ctx.enter_context(tc.psum_pool(name="psum_feat", bufs=4))
        psum_tok = ctx.enter_context(tc.psum_pool(name="psum_tok", bufs=4))
        ctx.enter_context(tc.manual_schedule())

        zeros = keep.tile([P, TOKENS], BF16, name="zeros")
        nc.gpsimd.memset(zeros[:], 0.0)

        def keep_warm(count):
            for n in range(count):
                unread = psum_tok.tile([P, TOKENS], F32, tag="bank", name="unread")
                nc.tensor.matmul(out=unread[:], lhsT=zeros[:, 0:P], rhs=zeros[:], start=True, stop=True)

        keep_warm(WARM_FIRST)
        bias_rows = keep.tile([P, P], BF16, name="bias_rows")
        nc.gpsimd.memset(bias_rows[:], 0.0)
        ident = keep.tile([P, P], F32, name="ident")
        make_identity(nc, ident[:])

        w_planes = keep.tile([P, PASSES, COLS], U8, name="w_planes", align_bytes=64)
        nc.vector.memset(w_planes[:].rearrange("p g n -> p (g n)").bitcast(I32), 0)

        nc.scalar.dma_start(out=bias_rows[0:COL_TILES, :], in_=qkv_b.rearrange("(c d) -> c d", d=P))
        wide = WIDE_HEADS * HEAD_DIM
        v_bias_row = keep.tile([P, wide], BF16, name="v_bias_row")
        nc.vector.memset(v_bias_row[:], 0.0)
        ones = keep.tile([P, P], BF16, name="ones")
        nc.vector.memset(ones[:], 1.0)
        cos_rows = keep.tile([P, TOK, HEAD_DIM], BF16, name="cos_rows")
        sin_rows = keep.tile([P, TOK, HEAD_DIM], BF16, name="sin_rows")

        def load_tables():
            nc.sync.dma_start(out=cos_rows[:], in_=rope_cos[0, 0].rearrange("(p j) d -> p j d", j=TOK))
            nc.sync.dma_start(out=sin_rows[:], in_=rope_sin[0, 0].rearrange("(p j) d -> p j d", j=TOK))

        x_rows = [keep.tile([P, PASSES, TOK, K_PASS], BF16, name="x_rows%d" % b) for b in range(BATCH)]

        def load_x(b):
            rows = x[b].rearrange("(p j) k -> p j k", j=TOK)
            for g in range(PASSES):
                of_pass = slice(K_PASS * g, K_PASS * (g + 1))
                for pair in range(PAIRS):
                    two = slice(2 * pair, 2 * pair + 2)
                    nc.sync.dma_start(out=x_rows[b][:, g, two, :], in_=rows[:, two, of_pass])

        def load_w_scales():
            rows = qkv_w_scales.rearrange("g q n -> q g n")
            for r in range(PACK):
                nc.sync.dma_start(out=w_planes[r:P:32, :, :].bitcast(I32), in_=rows[r : 4 * PACK : PACK, :, :].bitcast(I32))

        head_bytes = WORD_BYTES * HEAD_DIM
        w_words = [
            keep.tile([P, PASSES, STREAMS, HEADS_A_LOAD * head_bytes], U8, name="w_words%d" % part, align_bytes=64)
            for part in range(HEADS // HEADS_A_LOAD)
        ]

        w_wide = keep.tile([P, PASSES, WIDE_HEADS * head_bytes], U8, name="w_wide", align_bytes=64)

        def load_w_words(part):
            some = slice(HEADS_A_LOAD * head_bytes * part, HEADS_A_LOAD * head_bytes * (part + 1))
            streams = STREAMS if HEADS_A_LOAD * part < HEADS - WIDE_HEADS else STREAMS - 1
            for g in range(PASSES):
                there = qkv_w_words[g].rearrange("p (s c) -> p s c", s=STREAMS)
                nc.sync.dma_start(out=w_words[part][:, g, 0:streams, :].bitcast(I32), in_=there[:, 0:streams, some].bitcast(I32))

        def load_w_wide():
            for g in range(PASSES):
                nc.sync.dma_start(out=w_wide[:, g, :].bitcast(I32), in_=qkv_w_words[g][:, WORD_BYTES * (COLS - wide) : WORD_BYTES * COLS].bitcast(I32))

        load_x(0)
        load_w_scales()
        load_w_words(0)
        load_tables()
        nc.sync.dma_start(out=v_bias_row[0:1, :], in_=qkv_b[COLS - wide : COLS].rearrange("(o n) -> o n", o=1))
        load_x(1)
        load_w_words(1)
        load_w_wide()
        load_w_words(2)
        load_w_words(3)

        bias_rows_f32 = keep.tile([P, P], F32, name="bias_rows_f32")
        nc.gpsimd.tensor_copy(out=bias_rows_f32[:], in_=bias_rows[:])

        tables = keep.tile([P, TOK, 2, 2, HALF], BF16, name="tables")

        def make_tables():
            lo_cols = slice(0, HALF)
            hi_cols = slice(HALF, HEAD_DIM)
            nc.vector.tensor_copy(out=tables[:, :, 0, 0, :], in_=cos_rows[:, :, lo_cols])
            nc.vector.tensor_copy(out=tables[:, :, 0, 1, :], in_=sin_rows[:, :, hi_cols])
            nc.vector.tensor_scalar(out=tables[:, :, 1, 0, :], in0=sin_rows[:, :, lo_cols], scalar1=-1.0, scalar2=0.0, op0=MULT, op1=ADD)
            nc.vector.tensor_copy(out=tables[:, :, 1, 1, :], in_=cos_rows[:, :, hi_cols])

        grouped = [
            [keep.tile([P, PACK * TOKENS], BF16, name="grouped%d%d" % (b, g), align_bytes=64) for g in range(PASSES)]
            for b in range(BATCH)
        ]
        x_codes = keep.tile([P, BATCH, PASSES, TOKENS], U32, name="x_codes", align_bytes=64)
        x_planes = keep.tile([P, BATCH, PASSES, TOKENS], U8, name="x_planes", align_bytes=64)

        x_sorted = [keep.tile([P, PASSES, TOK, 2, P], F32, name="x_sorted%d" % b) for b in range(BATCH)]

        def sort_x(b, g, pair, copy):
            two = slice(2 * pair, 2 * pair + 2)
            words = x_rows[b][:, g, two, :].bitcast(F32)
            copy(out=x_sorted[b][:, g, two, :, :], in_=words.rearrange("t j (p u) -> t j u p", u=2))

        def transpose_x(b, g, pair, copy):
            xt = psum_feat.tile([P, 2, 2, P], F32, tag="bank", name="xt")
            for jj in range(2):
                for u in range(2):
                    nc.tensor.transpose(xt[:, jj, u, :], x_sorted[b][:, g, 2 * pair + jj, u, :], ident[:])
            pairs_of_k = grouped[b][g][:].bitcast(F32).rearrange("q (n u) -> q n u", u=2)
            columns = slice(2 * P * pair, 2 * P * (pair + 1))
            copy(
                out=pairs_of_k[:, columns, :].rearrange("q (jj n) u -> q jj n u", jj=2),
                in_=xt[:].rearrange("q jj u n -> q jj n u"),
            )

        def quantise_x(b, g, pair):
            columns = slice(2 * P * pair, 2 * P * (pair + 1))
            nc.vector.quantize_mx(
                out=x_codes[:, b, g, columns].bitcast(FP8X4),
                scales=x_planes[:, b, g, columns],
                in_=grouped[b][g][:, PACK * 2 * P * pair : PACK * 2 * P * (pair + 1)],
            )

        for pair in range(PAIRS):
            sort_x(0, 0, pair, nc.vector.tensor_copy)
            sort_x(0, 1, pair, nc.scalar.copy)
        for pair in range(PAIRS):
            transpose_x(0, 0, pair, nc.vector.tensor_copy)
            keep_warm(WARM_BETWEEN)
        for pair in range(PAIRS):
            transpose_x(0, 1, pair, nc.scalar.copy)
            keep_warm(WARM_BETWEEN)
            quantise_x(0, 0, pair)
        for pair in range(PAIRS):
            quantise_x(0, 1, pair)
        keep_warm(WARM_LAST)
        make_tables()
        for g in range(PASSES):
            for pair in range(PAIRS):
                sort_x(1, g, pair, nc.vector.tensor_copy)

        bias_t = psum_tok.tile([P, P], F32, tag="bank", name="bias_t")
        nc.tensor.transpose(bias_t[:], bias_rows_f32[:], ident[:])
        bias_col = keep.tile([P, COL_TILES], F32, name="bias_col")
        nc.scalar.copy(out=bias_col[:], in_=bias_t[:, 0:COL_TILES])

        def project(units):
            sums = [psum_feat.tile([P, TOKENS], F32, tag="bank", name="acc") for unit in units]
            for g in range(PASSES):
                for (s, b, h), acc in zip(units, sums):
                    c = s * HEADS + h
                    of_head = slice(head_bytes * (h % HEADS_A_LOAD), head_bytes * (h % HEADS_A_LOAD + 1))
                    nc.tensor.matmul_mx(
                        out=acc[:],
                        lhsT=w_words[h // HEADS_A_LOAD][:, g, s, of_head].bitcast(FP4X4),
                        lhsT_scale=w_planes[:, g, P * c : P * (c + 1)],
                        rhs=x_codes[:, b, g, :].bitcast(FP8X4),
                        rhs_scale=x_planes[:, b, g, :],
                        start=(g == 0),
                        stop=(g == PASSES - 1),
                    )
            biased = []
            for (s, b, h), acc in zip(units, sums):
                c = s * HEADS + h
                feat = feature_major.tile([P, TOKENS], F32, name="feat")
                nc.scalar.activation(out=feat[:], in_=acc[:], func=IDENTITY, bias=bias_col[:, c : c + 1])
                biased.append(feat)
            return biased

        def store(unit, result, queue):
            s, b, h = unit
            queue.dma_start(out=outs[s][b, h].rearrange("(p j) d -> p (j d)", j=TOK), in_=result)

        def finish(units, biased, adders):
            token_major = []
            for feat in biased:
                tok = psum_tok.tile([P, TOK, HEAD_DIM], F32, tag="bank", name="tok")
                for j in range(TOK):
                    nc.tensor.transpose(tok[:, j, :], feat[:, P * j : P * (j + 1)], ident[:])
                token_major.append(tok)

            plain = [(unit, tok) for unit, tok in zip(units, token_major) if unit[0] == 2]
            for unit, tok in plain:
                v_out = results.tile([P, TOK, HEAD_DIM], F32, name="v_out")
                nc.scalar.copy(out=v_out[:], in_=tok[:])
                store(unit, v_out[:].rearrange("p j d -> p (j d)"), nc.scalar)

            to_rotate = [(unit, tok) for unit, tok in zip(units, token_major) if unit[0] != 2]
            waiting = []
            for (unit, tok), adder in zip(to_rotate, adders):
                parts = products.tile([P, 2, TOK, HEAD_DIM], F32, name="parts")
                halves = tok[:].rearrange("p j (s i) -> p j s i", s=2)
                nc.vector.tensor_tensor(
                    out=parts[:].rearrange("p s j (w i) -> p j s w i", w=2),
                    in0=halves.unsqueeze(3).to_broadcast([P, TOK, 2, 2, HALF]),
                    in1=tables[:],
                    op=MULT,
                )
                waiting.append((unit, parts, adder))
            for unit, parts, adder in waiting:
                rotated = sums_pool.tile([P, TOK, HEAD_DIM], F32, name="rotated")
                adder.tensor_tensor(out=rotated[:], in0=parts[:, 0], in1=parts[:, 1], op=ADD)
                store(unit, rotated[:].rearrange("p j d -> p (j d)"), nc.sync)

        def project_wide(b, j):
            acc = psum_feat.tile([P, WIDE_HEADS, HEAD_DIM], F32, tag="bank", name="wide_acc")
            tokens = slice(P * j, P * (j + 1))
            for g in range(PASSES):
                nc.tensor.matmul_mx(
                    out=acc[:].rearrange("p h d -> p (h d)"),
                    lhsT=x_codes[:, b, g, tokens].bitcast(FP8X4),
                    lhsT_scale=x_planes[:, b, g, tokens],
                    rhs=w_wide[:, g, :].bitcast(FP4X4),
                    rhs_scale=w_planes[:, g, COLS - wide : COLS],
                    start=(g == 0),
                    stop=(g == PASSES - 1),
                )
            return acc

        wide_groups = {}

        def finish_wide(b, j, acc):
            if j == 0:
                wide_group = v_pool.tile([P, WIDE_HEADS, TOK, HEAD_DIM], F32, name="wide_group")
                wide_groups[b] = wide_group
            group = wide_groups[b]
            nc.vector.tensor_tensor(out=group[:, :, j, :], in0=acc[:], in1=v_bias[:], op=ADD)
            there = out_2[b, HEADS - WIDE_HEADS : HEADS]
            if b == BATCH - 1:
                nc.sync.dma_start(out=there.rearrange("h (p j) d -> p h j d", j=TOK)[:, :, j, :], in_=group[:, :, j, :])
            elif j == TOK - 1:
                nc.sync.dma_start(out=there.rearrange("h (p j) d -> p h (j d)", j=TOK), in_=group[:].rearrange("p h j d -> p h (j d)"))

        heads = [(b, h) for b in range(BATCH) for h in range(HEADS)]
        steps = [[(0, b, h), (1, b, h)] for b, h in heads] + [[]]
        wide_of_step = [[] for step in steps]
        for n in range(BATCH * TOK):
            wide_of_step[2 * n + 1].append((n // TOK, n % TOK))
            steps[2 * n + 2].append((2, n // TOK, n % TOK))
        x_banks = [(g, pair) for g in range(PASSES) for pair in range(PAIRS)]
        banks_a_step = len(x_banks) // V_LAG

        biased = project(steps[0])
        spread = psum_tok.tile([P, wide], F32, tag="bank", name="spread")
        nc.tensor.matmul(out=spread[:], lhsT=ones[:], rhs=v_bias_row[:], start=True, stop=True)
        v_bias = keep.tile([P, WIDE_HEADS, HEAD_DIM], F32, name="v_bias")
        nc.scalar.copy(out=v_bias[:].rearrange("p h d -> p (h d)"), in_=spread[:])
        for r in range(len(steps)):
            following = project(steps[r + 1]) if r + 1 < len(steps) else None
            for b, j in wide_of_step[r]:
                finish_wide(b, j, project_wide(b, j))
            finish(steps[r], biased, (nc.gpsimd, nc.vector if r + 1 >= len(heads) else nc.gpsimd))
            if r < V_LAG:
                for g, pair in x_banks[banks_a_step * r : banks_a_step * (r + 1)]:
                    transpose_x(1, g, pair, nc.scalar.copy)
                    quantise_x(1, g, pair)
            biased = following
